import numpy as np
import ml_dtypes


def mxq(x, axis, fmt="e4m3"):
    dtype, down = {"e4m3": (ml_dtypes.float8_e4m3fn, 7), "e5m2": (ml_dtypes.float8_e5m2, 14)}[fmt]
    v = np.moveaxis(np.asarray(x, np.float32).astype(ml_dtypes.bfloat16).astype(np.float64), axis, -1)
    blocks = v.reshape(v.shape[:-1] + (-1, 32))
    amax = np.abs(blocks).max(-1, keepdims=True)
    byte = np.maximum(np.where(amax > 0, np.frexp(amax)[1] - 1 + 127, 0) - down, 1)
    scale = np.exp2(byte - 127.0)
    codes = (blocks / scale).astype(np.float32).astype(dtype).astype(np.float64)
    return np.moveaxis((codes * scale).reshape(v.shape), -1, axis)


WIDE = False


def mx_kscale(k):
    if not WIDE:
        return np.ones(k)
    levels = np.array([10, -10, 5, -5, 0])
    if k % 512:
        return np.exp2(np.random.permutation(np.resize(levels, k // 32))).repeat(32)
    a = np.empty((k // 512, 16))
    for p in range(k // 512):
        a[p, :8] = np.random.permutation(np.resize(levels, 8))
        for g in range(8):
            far = levels[np.abs(levels - a[p, g]) >= 10]
            a[p, g + 8] = far[np.random.randint(len(far))]
    return np.exp2(a.ravel()).repeat(32)


BF16 = ml_dtypes.bfloat16


def bf(x):
    return np.asarray(x, np.float32).astype(BF16)


def f64(x):
    return np.asarray(x).astype(np.float64)


B, C, K, BK, BN = 1024, 2048, 2048, 1, 16
KEEP = 0.3


def setup_inputs():
    s = mx_kscale(C)
    x = np.random.standard_normal((B, C)) * s
    weight = np.random.uniform(-1.0, 1.0, (K, C)) * 3.2 / np.sqrt(C)
    blk = (np.random.uniform(0.0, 1.0, (K // BK, C // BN)) < KEEP).astype(np.float64)
    mask = np.repeat(np.repeat(blk, BK, axis=0), BN, axis=1)
    weight = weight * mask / s[None, :]
    bias = np.random.uniform(-1.0, 1.0, K) * 0.5
    return {"x": bf(x), "weight": bf(weight), "bias": bf(bias)}


def reference(x, weight, bias):
    return np.maximum((mxq(f64(x), 1, "e4m3") @ mxq(f64(weight), 1, "e4m3").T) + f64(bias), 0.0)

@@ -1,0 +1,217 @@
+from contextlib import ExitStack
+
+import concourse.mybir as mybir
+from concourse.masks import make_identity
+
+F32 = mybir.dt.float32
+BF16 = mybir.dt.bfloat16
+I32 = mybir.dt.int32
+U32 = mybir.dt.uint32
+U8 = mybir.dt.uint8
+FP8X4 = mybir.dt.float8_e4m3fn_x4
+ADD = mybir.AluOpType.add
+RELU = mybir.ActivationFunctionType.Relu
+
+P = 128
+B, C, K = 1024, 2048, 2048
+FLOPS = 2 * B * C * K
+
+M_TILES = B // P
+CHUNK = 512
+HALF = CHUNK // 2
+N_CHUNKS = K // CHUNK
+PASSES = C // 512
+WARM_START = 8
+WARM_PER_RUN = 3
+
+
+def tile_sparselinearrelu_kernel(tc, x, weight, bias, out):
+    nc = tc.nc
+    with ExitStack() as ctx:
+        ctx.enter_context(tc.manual_schedule())
+        keep = ctx.enter_context(tc.tile_pool(name="keep", bufs=1))
+        grp_pool = ctx.enter_context(tc.tile_pool(name="grp", bufs=8))
+        st_pool = ctx.enter_context(tc.tile_pool(name="st", bufs=16))
+        tp_pool = ctx.enter_context(tc.psum_pool(name="tp", bufs=4))
+        acc_pool = ctx.enter_context(tc.psum_pool(name="acc", bufs=4))
+
+        x_view = x.rearrange("(p t) k -> p t k", t=M_TILES)
+        out_view = out.rearrange("(p t) n -> t p n", t=M_TILES)
+        w_view = weight.rearrange("(j p) k -> p j k", p=P)
+
+        ones = keep.tile([P, CHUNK], BF16, name="ones")
+        nc.vector.memset(ones[:], 1.0)
+        brow = keep.tile([P, K], BF16, name="brow")
+        nc.vector.memset(brow[:].bitcast(I32), 0)
+        ident = keep.tile([P, P], F32, name="ident")
+        make_identity(nc, ident[:])
+
+        w_sb = {}
+        x_sb = {}
+
+        def load_w(c, h):
+            t = keep.tile([P, 2, C], BF16, name="w_sb_%d_%d" % (c, h))
+            j0 = 4 * c + 2 * h
+            nc.sync.dma_start(out=t[:], in_=w_view[:, j0:j0 + 2, :])
+            w_sb[(c, h)] = t
+
+        def load_x(i):
+            t = keep.tile([P, 2, C], BF16, name="x_sb_%d" % i)
+            nc.sync.dma_start(out=t[:], in_=x_view[:, 2 * i:2 * i + 2, :])
+            x_sb[i] = t
+
+        load_w(0, 0)
+        nc.sync.dma_start(out=brow[0:1, :], in_=bias.rearrange("(o n) -> o n", o=1))
+        load_x(0)
+        load_w(0, 1)
+        for i in range(1, 4):
+            load_x(i)
+        for c in range(1, N_CHUNKS):
+            load_w(c, 0)
+            load_w(c, 1)
+
+        xq = [keep.tile([P, PASSES * P], U32, name="xq_%d" % m, align_bytes=64) for m in range(M_TILES)]
+        xs = [keep.tile([P, PASSES * P], U8, name="xs_%d" % m, align_bytes=64) for m in range(M_TILES)]
+        wq = [[keep.tile([P, CHUNK], U32, name="wq_%d_%d" % (c, g), align_bytes=64) for g in range(PASSES)]
+              for c in range(N_CHUNKS)]
+        ws = [[keep.tile([P, CHUNK], U8, name="ws_%d_%d" % (c, g), align_bytes=64) for g in range(PASSES)]
+              for c in range(N_CHUNKS)]
+        bias_bc = keep.tile([P, K], F32, name="bias_bc")
+
+        def warm(n):
+            for i in range(n):
+                wacc = acc_pool.tile([P, CHUNK], F32, name="acc")
+                nc.tensor.matmul(out=wacc[:], lhsT=ones[:, 0:P], rhs=ones[:], start=True, stop=True)
+
+        def bias_matmul(c):
+            bacc = acc_pool.tile([P, CHUNK], F32, name="acc")
+            nc.tensor.matmul(out=bacc[:], lhsT=ones[:, 0:P], rhs=brow[:, c * CHUNK:(c + 1) * CHUNK],
+                             start=True, stop=True)
+            return bacc
+
+        def w_unit(c, h, g):
+            srcs = [w_sb[(c, h)][:, j, :].bitcast(F32)[:, 256 * g:256 * g + 256] for j in range(2)]
+            cols = slice(HALF * h, HALF * h + HALF)
+            return srcs, wq[c][g][:, cols], ws[c][g][:, cols]
+
+        def x_unit(m, gp):
+            row = x_sb[m // 2][:, m % 2, :].bitcast(F32)
+            srcs = [row[:, 256 * (2 * gp + a):256 * (2 * gp + a) + 256] for a in range(2)]
+            cols = slice(256 * gp, 256 * gp + 256)
+            return srcs, xq[m][:, cols], xs[m][:, cols]
+
+        def transposes(unit):
+            bank = tp_pool.tile([P, 2, 2, P], F32, name="bank")
+            for a in range(2):
+                for u in range(2):
+                    nc.tensor.transpose(bank[:, a, u, :], unit[0][a][:, u:256:2], ident[:])
+            return bank
+
+        def leave(engine_copy, bank):
+            grouped = grp_pool.tile([P, 1024], BF16, name="grouped", align_bytes=64)
+            engine_copy(
+                out=grouped[:].bitcast(F32).rearrange("p (a c u) -> p a c u", a=2, u=2),
+                in_=bank[:].rearrange("p a u c -> p a c u"),
+            )
+            return grouped
+
+        def quantise(unit, grouped):
+            nc.vector.quantize_mx(out=unit[1].bitcast(FP8X4), scales=unit[2], in_=grouped[:])
+
+        def passes(acc, m, c, lo, width):
+            for g in range(PASSES):
+                cols = slice(P * g, P * g + P)
+                nc.tensor.matmul_mx(
+                    out=acc[:, lo:lo + width],
+                    lhsT=xq[m][:, cols].bitcast(FP8X4),
+                    lhsT_scale=xs[m][:, cols],
+                    rhs=wq[c][g][:, lo:lo + width].bitcast(FP8X4),
+                    rhs_scale=ws[c][g][:, lo:lo + width],
+                    start=(g == 0),
+                    stop=(g == PASSES - 1),
+                )
+
+        def add_bias(done):
+            acc, m, c, lo, width = done
+            st = st_pool.tile([P, CHUNK], F32, name="st")
+            nc.vector.tensor_tensor(out=st[:, 0:width], in0=acc[:, lo:lo + width],
+                                    in1=bias_bc[:, c * CHUNK + lo:c * CHUNK + lo + width], op=ADD)
+            return st, m, c, lo, width
+
+        def relu_store(summed):
+            st, m, c, lo, width = summed
+            nc.scalar.activation(out=st[:, 0:width], in_=st[:, 0:width], func=RELU)
+            nc.sync.dma_start(out=out_view[m][:, c * CHUNK + lo:c * CHUNK + lo + width], in_=st[:, 0:width])
+
+        def w_run(c, h):
+            return [w_unit(c, h, g) for g in range(PASSES)]
+
+        def x_run(i):
+            return [x_unit(2 * i + s, gp) for s in range(2) for gp in range(2)]
+
+        def whole(ms, c):
+            return [(m, c, 0, CHUNK, "whole") for m in ms]
+
+        cycles = [
+            (w_run(0, 0), "warm", []),
+            (x_run(0), "bias", []),
+            (w_run(0, 1), "", [(0, 0, 0, HALF, "first"), (1, 0, 0, HALF, "first")]),
+            (x_run(1), "", [(0, 0, HALF, HALF, "second"), (1, 0, HALF, HALF, "second")]),
+            (x_run(2), "", whole([2, 3], 0)),
+            (x_run(3), "", whole([4, 5], 0)),
+            (w_run(1, 0), "", whole([6], 0)),
+            (w_run(1, 1), "", whole([7], 0)),
+            (w_run(2, 0), "", whole(range(0, 4), 1)),
+            (w_run(2, 1), "", whole(range(4, 8), 1)),
+            (w_run(3, 0), "", whole(range(0, 4), 2)),
+            (w_run(3, 1), "", whole(range(4, 8), 2)),
+            ([], "", whole(range(0, 7), 3) + [(7, 3, 0, HALF, "part"), (7, 3, HALF, HALF, "part")]),
+        ]
+
+        warm(WARM_START)
+        waiting = None
+        pending = []
+        held = {}
+        for run, plain, block in cycles:
+            banks = [transposes(unit) for unit in run]
+            baccs = []
+            if plain == "warm":
+                warm(WARM_PER_RUN)
+            if plain == "bias":
+                baccs = [bias_matmul(c) for c in range(N_CHUNKS)]
+            if waiting is not None:
+                pending.append(add_bias(waiting))
+                waiting = None
+            tiles = [leave(nc.scalar.copy, bank) for bank in banks[0:3]]
+            for summed in pending:
+                relu_store(summed)
+            pending = []
+            if run:
+                quantise(run[0], tiles[0])
+                tiles.append(leave(nc.vector.tensor_copy, banks[3]))
+                quantise(run[1], tiles[1])
+                quantise(run[2], tiles[2])
+                quantise(run[3], tiles[3])
+            for c, bacc in enumerate(baccs):
+                copy = nc.scalar.copy if c % 2 == 0 else nc.vector.tensor_copy
+                copy(out=bias_bc[:, c * CHUNK:(c + 1) * CHUNK], in_=bacc[:])
+            for m, c, lo, width, kind in block:
+                if waiting is not None:
+                    pending.append(add_bias(waiting))
+                    waiting = None
+                if not run:
+                    for summed in pending:
+                        relu_store(summed)
+                    pending = []
+                if kind == "second":
+                    acc = held[(m, c)]
+                else:
+                    acc = acc_pool.tile([P, CHUNK], F32, name="acc")
+                passes(acc, m, c, lo, width)
+                if kind == "first":
+                    held[(m, c)] = acc
+                elif kind == "second":
+                    waiting = (acc, m, c, 0, CHUNK)
+                else:
+                    waiting = (acc, m, c, lo, width)
+        relu_store(add_bias(waiting))

@@ -31,6 +31,7 @@ def tile_sparselinearrelu_kernel(tc, x, weight, bias, out):
         ctx.enter_context(tc.manual_schedule())
         keep = ctx.enter_context(tc.tile_pool(name="keep", bufs=1))
         grp_pool = ctx.enter_context(tc.tile_pool(name="grp", bufs=8))
+        perm_pool = ctx.enter_context(tc.tile_pool(name="permp", bufs=4))
         st_pool = ctx.enter_context(tc.tile_pool(name="st", bufs=16))
         tp_pool = ctx.enter_context(tc.psum_pool(name="tp", bufs=4))
         acc_pool = ctx.enter_context(tc.psum_pool(name="acc", bufs=4))
@@ -47,6 +48,7 @@ def tile_sparselinearrelu_kernel(tc, x, weight, bias, out):
         make_identity(nc, ident[:])
 
         w_sb = {}
+        perm = {}
         x_sb = {}
 
         def load_w(c, h):
@@ -89,14 +91,27 @@ def tile_sparselinearrelu_kernel(tc, x, weight, bias, out):
                              start=True, stop=True)
             return bacc
 
+        def regroup(c, h, j):
+            t = perm_pool.tile([P, C], BF16, name="perm", align_bytes=64)
+            nc.vector.tensor_copy(
+                out=t[:].bitcast(F32).rearrange("p (g u c) -> p g u c", g=PASSES, u=2),
+                in_=w_sb[(c, h)][:, j, :].bitcast(F32).rearrange("p (g c u) -> p g u c", g=PASSES, u=2),
+            )
+            perm[(c, h, j)] = t
+
+        def words(c, h, j, g, u):
+            if (c, h, j) in perm:
+                return perm[(c, h, j)][:].bitcast(F32)[:, 256 * g + P * u:256 * g + P * u + P]
+            return w_sb[(c, h)][:, j, :].bitcast(F32)[:, 256 * g + u:256 * g + 256:2]
+
         def w_unit(c, h, g):
-            srcs = [w_sb[(c, h)][:, j, :].bitcast(F32)[:, 256 * g:256 * g + 256] for j in range(2)]
+            srcs = [[words(c, h, j, g, u) for u in range(2)] for j in range(2)]
             cols = slice(HALF * h, HALF * h + HALF)
             return srcs, wq[c][g][:, cols], ws[c][g][:, cols]
 
         def x_unit(m, gp):
             row = x_sb[m // 2][:, m % 2, :].bitcast(F32)
-            srcs = [row[:, 256 * (2 * gp + a):256 * (2 * gp + a) + 256] for a in range(2)]
+            srcs = [[row[:, 256 * (2 * gp + a) + u:256 * (2 * gp + a) + 256:2] for u in range(2)] for a in range(2)]
             cols = slice(256 * gp, 256 * gp + 256)
             return srcs, xq[m][:, cols], xs[m][:, cols]
 
@@ -104,7 +119,7 @@ def tile_sparselinearrelu_kernel(tc, x, weight, bias, out):
             bank = tp_pool.tile([P, 2, 2, P], F32, name="bank")
             for a in range(2):
                 for u in range(2):
-                    nc.tensor.transpose(bank[:, a, u, :], unit[0][a][:, u:256:2], ident[:])
+                    nc.tensor.transpose(bank[:, a, u, :], unit[0][a][u], ident[:])
             return bank
 
         def leave(engine_copy, bank):
@@ -153,26 +168,29 @@ def tile_sparselinearrelu_kernel(tc, x, weight, bias, out):
             return [(m, c, 0, CHUNK, "whole") for m in ms]
 
         cycles = [
-            (w_run(0, 0), "warm", []),
-            (x_run(0), "bias", []),
-            (w_run(0, 1), "", [(0, 0, 0, HALF, "first"), (1, 0, 0, HALF, "first")]),
-            (x_run(1), "", [(0, 0, HALF, HALF, "second"), (1, 0, HALF, HALF, "second")]),
-            (x_run(2), "", whole([2, 3], 0)),
-            (x_run(3), "", whole([4, 5], 0)),
-            (w_run(1, 0), "", whole([6], 0)),
-            (w_run(1, 1), "", whole([7], 0)),
-            (w_run(2, 0), "", whole(range(0, 4), 1)),
-            (w_run(2, 1), "", whole(range(4, 8), 1)),
-            (w_run(3, 0), "", whole(range(0, 4), 2)),
-            (w_run(3, 1), "", whole(range(4, 8), 2)),
-            ([], "", whole(range(0, 7), 3) + [(7, 3, 0, HALF, "part"), (7, 3, HALF, HALF, "part")]),
+            (w_run, (0, 0), "warm", []),
+            (x_run, (0,), "bias", []),
+            (w_run, (0, 1), "", [(0, 0, 0, HALF, "first"), (1, 0, 0, HALF, "first")]),
+            (x_run, (1,), "", [(0, 0, HALF, HALF, "second"), (1, 0, HALF, HALF, "second")]),
+            (x_run, (2,), "", whole([2, 3], 0)),
+            (x_run, (3,), "", whole([4, 5], 0)),
+            (w_run, (1, 0), "", whole([6], 0)),
+            (w_run, (1, 1), "", whole([7], 0)),
+            (w_run, (2, 0), "", whole(range(0, 4), 1)),
+            (w_run, (2, 1), "", whole(range(4, 8), 1)),
+            (w_run, (3, 0), "", whole(range(0, 4), 2)),
+            (w_run, (3, 1), "", whole(range(4, 8), 2)),
+            (None, (), "", whole(range(0, 7), 3) + [(7, 3, 0, HALF, "part"), (7, 3, HALF, HALF, "part")]),
         ]
 
         warm(WARM_START)
         waiting = None
         pending = []
         held = {}
-        for run, plain, block in cycles:
+        ahead = {6: (1, 1), 7: (2, 0), 8: (2, 1), 9: (3, 0), 10: (3, 1)}
+        for n, (make, args, plain, block) in enumerate(cycles):
+            run = make(*args) if make else []
+            todo = [ahead[n] + (j,) for j in range(2)] if n in ahead else []
             banks = [transposes(unit) for unit in run]
             baccs = []
             if plain == "warm":
@@ -195,10 +213,14 @@ def tile_sparselinearrelu_kernel(tc, x, weight, bias, out):
             for c, bacc in enumerate(baccs):
                 copy = nc.scalar.copy if c % 2 == 0 else nc.vector.tensor_copy
                 copy(out=bias_bc[:, c * CHUNK:(c + 1) * CHUNK], in_=bacc[:])
+            if todo:
+                regroup(*todo.pop(0))
             for m, c, lo, width, kind in block:
                 if waiting is not None:
                     pending.append(add_bias(waiting))
                     waiting = None
+                    if todo:
+                        regroup(*todo.pop(0))
                 if not run:
                     for summed in pending:
                         relu_store(summed)
@@ -214,4 +236,6 @@ def tile_sparselinearrelu_kernel(tc, x, weight, bias, out):
                     waiting = (acc, m, c, 0, CHUNK)
                 else:
                     waiting = (acc, m, c, lo, width)
+            for item in todo:
+                regroup(*item)
         relu_store(add_bias(waiting))

@@ -47,30 +47,25 @@ def tile_sparselinearrelu_kernel(tc, x, weight, bias, out):
         ident = keep.tile([P, P], F32, name="ident")
         make_identity(nc, ident[:])
 
-        w_sb = {}
-        perm = {}
-        x_sb = {}
+        raw = {}
 
-        def load_w(c, h):
-            t = keep.tile([P, 2, C], BF16, name="w_sb_%d_%d" % (c, h))
-            j0 = 4 * c + 2 * h
-            nc.sync.dma_start(out=t[:], in_=w_view[:, j0:j0 + 2, :])
-            w_sb[(c, h)] = t
+        def load(kind, first, count, parts=1):
+            view = x_view if kind == "x" else w_view
+            width = C // parts
+            for i in range(parts):
+                t = keep.tile([P, count, width], BF16, name="%s_sb_%d_%d" % (kind, first, i))
+                nc.sync.dma_start(out=t[:], in_=view[:, first:first + count, width * i:width * i + width])
+                for j in range(count):
+                    raw.setdefault((kind, first + j), []).append(t[:, j, :])
 
-        def load_x(i):
-            t = keep.tile([P, 2, C], BF16, name="x_sb_%d" % i)
-            nc.sync.dma_start(out=t[:], in_=x_view[:, 2 * i:2 * i + 2, :])
-            x_sb[i] = t
-
-        load_w(0, 0)
-        nc.sync.dma_start(out=brow[0:1, :], in_=bias.rearrange("(o n) -> o n", o=1))
-        load_x(0)
-        load_w(0, 1)
+        load("w", 0, 2, 2)
+        nc.scalar.dma_start(out=brow[0:1, :], in_=bias.rearrange("(o n) -> o n", o=1))
+        load("x", 0, 2, 2)
+        load("w", 2, 2)
         for i in range(1, 4):
-            load_x(i)
-        for c in range(1, N_CHUNKS):
-            load_w(c, 0)
-            load_w(c, 1)
+            load("x", 2 * i, 2)
+        for j in range(4, 16, 2):
+            load("w", j, 2)
 
         xq = [keep.tile([P, PASSES * P], U32, name="xq_%d" % m, align_bytes=64) for m in range(M_TILES)]
         xs = [keep.tile([P, PASSES * P], U8, name="xs_%d" % m, align_bytes=64) for m in range(M_TILES)]
@@ -91,35 +86,40 @@ def tile_sparselinearrelu_kernel(tc, x, weight, bias, out):
                              start=True, stop=True)
             return bacc
 
-        def regroup(c, h, j):
-            t = perm_pool.tile([P, C], BF16, name="perm", align_bytes=64)
-            nc.vector.tensor_copy(
-                out=t[:].bitcast(F32).rearrange("p (g u c) -> p g u c", g=PASSES, u=2),
-                in_=w_sb[(c, h)][:, j, :].bitcast(F32).rearrange("p (g c u) -> p g u c", g=PASSES, u=2),
-            )
-            perm[(c, h, j)] = t
+        perm = {}
 
-        def words(c, h, j, g, u):
-            if (c, h, j) in perm:
-                return perm[(c, h, j)][:].bitcast(F32)[:, 256 * g + P * u:256 * g + P * u + P]
-            return w_sb[(c, h)][:, j, :].bitcast(F32)[:, 256 * g + u:256 * g + 256:2]
+        def regroup(engine_copy, key):
+            t = perm_pool.tile([P, C], BF16, name="perm", align_bytes=64)
+            engine_copy(
+                out=t[:].bitcast(F32).rearrange("p (g u c) -> p g u c", g=PASSES, u=2),
+                in_=raw[key][0].bitcast(F32).rearrange("p (g c u) -> p g u c", g=PASSES, u=2),
+            )
+            perm[key] = t
+
+        def words(key, g, u):
+            if key in perm:
+                return perm[key][:].bitcast(F32)[:, 256 * g + P * u:256 * g + P * u + P]
+            parts = raw[key]
+            per_part = PASSES // len(parts)
+            lo = 256 * (g % per_part)
+            return parts[g // per_part].bitcast(F32)[:, lo + u:lo + 256:2]
 
         def w_unit(c, h, g):
-            srcs = [[words(c, h, j, g, u) for u in range(2)] for j in range(2)]
+            srcs = [("w", 4 * c + 2 * h + j, g) for j in range(2)]
             cols = slice(HALF * h, HALF * h + HALF)
             return srcs, wq[c][g][:, cols], ws[c][g][:, cols]
 
         def x_unit(m, gp):
-            row = x_sb[m // 2][:, m % 2, :].bitcast(F32)
-            srcs = [[row[:, 256 * (2 * gp + a) + u:256 * (2 * gp + a) + 256:2] for u in range(2)] for a in range(2)]
+            srcs = [("x", m, 2 * gp + a) for a in range(2)]
             cols = slice(256 * gp, 256 * gp + 256)
             return srcs, xq[m][:, cols], xs[m][:, cols]
 
         def transposes(unit):
             bank = tp_pool.tile([P, 2, 2, P], F32, name="bank")
             for a in range(2):
+                kind, row, g = unit[0][a]
                 for u in range(2):
-                    nc.tensor.transpose(bank[:, a, u, :], unit[0][a][u], ident[:])
+                    nc.tensor.transpose(bank[:, a, u, :], words((kind, row), g, u), ident[:])
             return bank
 
         def leave(engine_copy, bank):
@@ -164,33 +164,37 @@ def tile_sparselinearrelu_kernel(tc, x, weight, bias, out):
         def x_run(i):
             return [x_unit(2 * i + s, gp) for s in range(2) for gp in range(2)]
 
+        def rows_of(run):
+            return sorted({(kind, row) for unit in run for kind, row, g in unit[0]})
+
+        def half(ms, c, h):
+            return [(m, c, HALF * h, HALF, "part") for m in ms]
+
         def whole(ms, c):
             return [(m, c, 0, CHUNK, "whole") for m in ms]
 
         cycles = [
-            (w_run, (0, 0), "warm", []),
-            (x_run, (0,), "bias", []),
-            (w_run, (0, 1), "", [(0, 0, 0, HALF, "first"), (1, 0, 0, HALF, "first")]),
-            (x_run, (1,), "", [(0, 0, HALF, HALF, "second"), (1, 0, HALF, HALF, "second")]),
-            (x_run, (2,), "", whole([2, 3], 0)),
-            (x_run, (3,), "", whole([4, 5], 0)),
-            (w_run, (1, 0), "", whole([6], 0)),
-            (w_run, (1, 1), "", whole([7], 0)),
-            (w_run, (2, 0), "", whole(range(0, 4), 1)),
-            (w_run, (2, 1), "", whole(range(4, 8), 1)),
-            (w_run, (3, 0), "", whole(range(0, 4), 2)),
-            (w_run, (3, 1), "", whole(range(4, 8), 2)),
-            (None, (), "", whole(range(0, 7), 3) + [(7, 3, 0, HALF, "part"), (7, 3, HALF, HALF, "part")]),
+            (w_run(0, 0), "bias", []),
+            (x_run(0), "", []),
+            (w_run(0, 1), "", half([0, 1], 0, 0)),
+            (x_run(1), "", half([0, 1], 0, 1)),
+            (x_run(2), "", whole([2, 3], 0)),
+            (x_run(3), "", whole([4, 5], 0)),
+            (w_run(1, 0), "", whole([6, 7], 0)),
+            (w_run(1, 1), "", half([0, 1, 2, 3], 1, 0)),
+            (w_run(2, 0), "", half([0, 1, 2, 3], 1, 1) + whole([4], 1)),
+            (w_run(2, 1), "", whole([5, 6, 7], 1)),
+            (w_run(3, 0), "", whole(range(0, 4), 2)),
+            (w_run(3, 1), "", whole(range(4, 8), 2)),
+            ([], "", whole(range(0, 7), 3) + [(7, 3, 0, HALF, "part"), (7, 3, HALF, HALF, "part")]),
         ]
 
         warm(WARM_START)
         waiting = None
         pending = []
         held = {}
-        ahead = {6: (1, 1), 7: (2, 0), 8: (2, 1), 9: (3, 0), 10: (3, 1)}
-        for n, (make, args, plain, block) in enumerate(cycles):
-            run = make(*args) if make else []
-            todo = [ahead[n] + (j,) for j in range(2)] if n in ahead else []
+        for n, (run, plain, block) in enumerate(cycles):
+            ahead = rows_of(cycles[n + 1][0]) if 3 <= n + 1 < len(cycles) else []
             banks = [transposes(unit) for unit in run]
             baccs = []
             if plain == "warm":
@@ -200,7 +204,11 @@ def tile_sparselinearrelu_kernel(tc, x, weight, bias, out):
             if waiting is not None:
                 pending.append(add_bias(waiting))
                 waiting = None
+            for key in ahead[0:1]:
+                regroup(nc.vector.tensor_copy, key)
             tiles = [leave(nc.scalar.copy, bank) for bank in banks[0:3]]
+            for key in ahead[1:2]:
+                regroup(nc.scalar.copy, key)
             for summed in pending:
                 relu_store(summed)
             pending = []
@@ -213,14 +221,10 @@ def tile_sparselinearrelu_kernel(tc, x, weight, bias, out):
             for c, bacc in enumerate(baccs):
                 copy = nc.scalar.copy if c % 2 == 0 else nc.vector.tensor_copy
                 copy(out=bias_bc[:, c * CHUNK:(c + 1) * CHUNK], in_=bacc[:])
-            if todo:
-                regroup(*todo.pop(0))
             for m, c, lo, width, kind in block:
                 if waiting is not None:
                     pending.append(add_bias(waiting))
                     waiting = None
-                    if todo:
-                        regroup(*todo.pop(0))
                 if not run:
                     for summed in pending:
                         relu_store(summed)
@@ -236,6 +240,4 @@ def tile_sparselinearrelu_kernel(tc, x, weight, bias, out):
                     waiting = (acc, m, c, 0, CHUNK)
                 else:
                     waiting = (acc, m, c, lo, width)
-            for item in todo:
-                regroup(*item)
         relu_store(add_bias(waiting))

@@ -40,12 +40,14 @@ def tile_sparselinearrelu_kernel(tc, x, weight, bias, out):
         out_view = out.rearrange("(p t) n -> t p n", t=M_TILES)
         w_view = weight.rearrange("(j p) k -> p j k", p=P)
 
+        brow = keep.tile([P, CHUNK], BF16, name="brow")
+        nc.vector.memset(brow[:].bitcast(I32), 0)
         ones = keep.tile([P, CHUNK], BF16, name="ones")
         nc.vector.memset(ones[:], 1.0)
-        brow = keep.tile([P, K], BF16, name="brow")
-        nc.vector.memset(brow[:].bitcast(I32), 0)
         ident = keep.tile([P, P], F32, name="ident")
         make_identity(nc, ident[:])
+        pick = keep.tile([P, N_CHUNKS], BF16, name="pick")
+        nc.vector.tensor_copy(out=pick[:], in_=ident[:, 0:N_CHUNKS])
 
         raw = {}
 
@@ -59,7 +61,7 @@ def tile_sparselinearrelu_kernel(tc, x, weight, bias, out):
                     raw.setdefault((kind, first + j), []).append(t[:, j, :])
 
         load("w", 0, 2, 2)
-        nc.scalar.dma_start(out=brow[0:1, :], in_=bias.rearrange("(o n) -> o n", o=1))
+        nc.sync.dma_start(out=brow[0:N_CHUNKS, :], in_=bias.rearrange("(o n) -> o n", o=N_CHUNKS))
         load("x", 0, 2, 2)
         load("w", 2, 2)
         for i in range(1, 4):
@@ -82,7 +84,7 @@ def tile_sparselinearrelu_kernel(tc, x, weight, bias, out):
 
         def bias_matmul(c):
             bacc = acc_pool.tile([P, CHUNK], F32, name="acc")
-            nc.tensor.matmul(out=bacc[:], lhsT=ones[:, 0:P], rhs=brow[:, c * CHUNK:(c + 1) * CHUNK],
+            nc.tensor.matmul(out=bacc[:], lhsT=pick[:, c:c + 1].to_broadcast([P, P]), rhs=brow[:],
                              start=True, stop=True)
             return bacc
 

@@ -21,8 +21,7 @@ CHUNK = 512
 HALF = CHUNK // 2
 N_CHUNKS = K // CHUNK
 PASSES = C // 512
-WARM_START = 8
-WARM_PER_RUN = 3
+WARM_START = 5
 
 
 def tile_sparselinearrelu_kernel(tc, x, weight, bias, out):
@@ -176,19 +175,19 @@ def tile_sparselinearrelu_kernel(tc, x, weight, bias, out):
             return [(m, c, 0, CHUNK, "whole") for m in ms]
 
         cycles = [
-            (w_run(0, 0), "bias", []),
-            (x_run(0), "", []),
-            (w_run(0, 1), "", half([0, 1], 0, 0)),
-            (x_run(1), "", half([0, 1], 0, 1)),
-            (x_run(2), "", whole([2, 3], 0)),
-            (x_run(3), "", whole([4, 5], 0)),
-            (w_run(1, 0), "", whole([6, 7], 0)),
-            (w_run(1, 1), "", half([0, 1, 2, 3], 1, 0)),
-            (w_run(2, 0), "", half([0, 1, 2, 3], 1, 1) + whole([4], 1)),
-            (w_run(2, 1), "", whole([5, 6, 7], 1)),
-            (w_run(3, 0), "", whole(range(0, 4), 2)),
-            (w_run(3, 1), "", whole(range(4, 8), 2)),
-            ([], "", whole(range(0, 7), 3) + [(7, 3, 0, HALF, "part"), (7, 3, HALF, HALF, "part")]),
+            (w_run(0, 0), [0, 1], []),
+            (x_run(0), [2, 3], []),
+            (w_run(0, 1), [], half([0, 1], 0, 0)),
+            (x_run(1), [], half([0, 1], 0, 1)),
+            (x_run(2), [], whole([2, 3], 0)),
+            (x_run(3), [], whole([4, 5], 0)),
+            (w_run(1, 0), [], whole([6, 7], 0)),
+            (w_run(1, 1), [], half([0, 1, 2, 3], 1, 0)),
+            (w_run(2, 0), [], half([0, 1, 2, 3], 1, 1) + whole([4], 1)),
+            (w_run(2, 1), [], whole([5, 6, 7], 1)),
+            (w_run(3, 0), [], whole(range(0, 4), 2)),
+            (w_run(3, 1), [], whole(range(4, 8), 2)),
+            ([], [], whole(range(0, 7), 3) + [(7, 3, 0, HALF, "part"), (7, 3, HALF, HALF, "part")]),
         ]
 
         warm(WARM_START)
@@ -199,10 +198,8 @@ def tile_sparselinearrelu_kernel(tc, x, weight, bias, out):
             ahead = rows_of(cycles[n + 1][0]) if 3 <= n + 1 < len(cycles) else []
             banks = [transposes(unit) for unit in run]
             baccs = []
-            if plain == "warm":
-                warm(WARM_PER_RUN)
-            if plain == "bias":
-                baccs = [bias_matmul(c) for c in range(N_CHUNKS)]
+            for c in plain:
+                baccs.append((c, bias_matmul(c)))
             if waiting is not None:
                 pending.append(add_bias(waiting))
                 waiting = None
@@ -220,7 +217,7 @@ def tile_sparselinearrelu_kernel(tc, x, weight, bias, out):
                 quantise(run[1], tiles[1])
                 quantise(run[2], tiles[2])
                 quantise(run[3], tiles[3])
-            for c, bacc in enumerate(baccs):
+            for c, bacc in baccs:
                 copy = nc.scalar.copy if c % 2 == 0 else nc.vector.tensor_copy
                 copy(out=bias_bc[:, c * CHUNK:(c + 1) * CHUNK], in_=bacc[:])
             for m, c, lo, width, kind in block:

@@ -30,8 +30,8 @@ def tile_sparselinearrelu_kernel(tc, x, weight, bias, out):
         ctx.enter_context(tc.manual_schedule())
         keep = ctx.enter_context(tc.tile_pool(name="keep", bufs=1))
         grp_pool = ctx.enter_context(tc.tile_pool(name="grp", bufs=8))
-        perm_pool = ctx.enter_context(tc.tile_pool(name="permp", bufs=4))
-        st_pool = ctx.enter_context(tc.tile_pool(name="st", bufs=16))
+        perm_pool = ctx.enter_context(tc.tile_pool(name="permp", bufs=6))
+        st_pool = ctx.enter_context(tc.tile_pool(name="st", bufs=14))
         tp_pool = ctx.enter_context(tc.psum_pool(name="tp", bufs=4))
         acc_pool = ctx.enter_context(tc.psum_pool(name="acc", bufs=4))
 
@@ -134,109 +134,141 @@ def tile_sparselinearrelu_kernel(tc, x, weight, bias, out):
         def quantise(unit, grouped):
             nc.vector.quantize_mx(out=unit[1].bitcast(FP8X4), scales=unit[2], in_=grouped[:])
 
-        def passes(acc, m, c, lo, width):
-            for g in range(PASSES):
-                cols = slice(P * g, P * g + P)
-                nc.tensor.matmul_mx(
-                    out=acc[:, lo:lo + width],
-                    lhsT=xq[m][:, cols].bitcast(FP8X4),
-                    lhsT_scale=xs[m][:, cols],
-                    rhs=wq[c][g][:, lo:lo + width].bitcast(FP8X4),
-                    rhs_scale=ws[c][g][:, lo:lo + width],
-                    start=(g == 0),
-                    stop=(g == PASSES - 1),
-                )
+        def multiply(group):
+            acc = acc_pool.tile([P, CHUNK], F32, name="acc")
+            at = 0
+            for m, c, lo, width in group:
+                for g in range(PASSES):
+                    cols = slice(P * g, P * g + P)
+                    nc.tensor.matmul_mx(
+                        out=acc[:, at:at + width],
+                        lhsT=xq[m][:, cols].bitcast(FP8X4),
+                        lhsT_scale=xs[m][:, cols],
+                        rhs=wq[c][g][:, lo:lo + width].bitcast(FP8X4),
+                        rhs_scale=ws[c][g][:, lo:lo + width],
+                        start=(g == 0),
+                        stop=(g == PASSES - 1),
+                    )
+                at += width
+            return acc, group
 
         def add_bias(done):
-            acc, m, c, lo, width = done
+            acc, group = done
+            m, c, lo, width = group[0]
+            n = len(group)
             st = st_pool.tile([P, CHUNK], F32, name="st")
-            nc.vector.tensor_tensor(out=st[:, 0:width], in0=acc[:, lo:lo + width],
-                                    in1=bias_bc[:, c * CHUNK + lo:c * CHUNK + lo + width], op=ADD)
-            return st, m, c, lo, width
+            nc.vector.tensor_tensor(
+                out=st[:, 0:n * width].rearrange("p (n w) -> p n w", n=n),
+                in0=acc[:, 0:n * width].rearrange("p (n w) -> p n w", n=n),
+                in1=bias_bc[:, c * CHUNK + lo:c * CHUNK + lo + width].unsqueeze(1).to_broadcast([P, n, width]),
+                op=ADD)
+            return st, group
 
         def relu_store(summed):
-            st, m, c, lo, width = summed
-            nc.scalar.activation(out=st[:, 0:width], in_=st[:, 0:width], func=RELU)
-            nc.sync.dma_start(out=out_view[m][:, c * CHUNK + lo:c * CHUNK + lo + width], in_=st[:, 0:width])
+            st, group = summed
+            total = sum(width for m, c, lo, width in group)
+            nc.scalar.activation(out=st[:, 0:total], in_=st[:, 0:total], func=RELU)
+            at = 0
+            for m, c, lo, width in group:
+                nc.sync.dma_start(out=out_view[m][:, c * CHUNK + lo:c * CHUNK + lo + width], in_=st[:, at:at + width])
+                at += width
 
-        def w_run(c, h):
+        def w_half(c, h):
             return [w_unit(c, h, g) for g in range(PASSES)]
 
-        def x_run(i):
-            return [x_unit(2 * i + s, gp) for s in range(2) for gp in range(2)]
-
-        def rows_of(run):
-            return sorted({(kind, row) for unit in run for kind, row, g in unit[0]})
-
-        def half(ms, c, h):
-            return [(m, c, HALF * h, HALF, "part") for m in ms]
+        def x_tile(m):
+            return [x_unit(m, gp) for gp in range(2)]
 
         def whole(ms, c):
-            return [(m, c, 0, CHUNK, "whole") for m in ms]
+            return [[(m, c, 0, CHUNK)] for m in ms]
 
-        cycles = [
-            (w_run(0, 0), [0, 1], []),
-            (x_run(0), [2, 3], []),
-            (w_run(0, 1), [], half([0, 1], 0, 0)),
-            (x_run(1), [], half([0, 1], 0, 1)),
-            (x_run(2), [], whole([2, 3], 0)),
-            (x_run(3), [], whole([4, 5], 0)),
-            (w_run(1, 0), [], whole([6, 7], 0)),
-            (w_run(1, 1), [], half([0, 1, 2, 3], 1, 0)),
-            (w_run(2, 0), [], half([0, 1, 2, 3], 1, 1) + whole([4], 1)),
-            (w_run(2, 1), [], whole([5, 6, 7], 1)),
-            (w_run(3, 0), [], whole(range(0, 4), 2)),
-            (w_run(3, 1), [], whole(range(4, 8), 2)),
-            ([], [], whole(range(0, 7), 3) + [(7, 3, 0, HALF, "part"), (7, 3, HALF, HALF, "part")]),
+        def pair(m, c, h):
+            return [[(m, c, HALF * h, HALF), (m + 1, c, HALF * h, HALF)]]
+
+        order = w_half(0, 0) + x_tile(0) + x_tile(1) + w_half(0, 1)
+        for m in range(2, M_TILES):
+            order += x_tile(m)
+        for c in range(1, N_CHUNKS):
+            order += w_half(c, 0) + w_half(c, 1)
+
+        runs = [order[i:i + 4] for i in range(0, 12, 4)] + [order[i:i + 3] for i in range(12, len(order), 3)]
+        blocks = [
+            [],
+            [],
+            pair(0, 0, 0),
+            pair(0, 0, 1),
+            whole([2], 0),
+            whole([3], 0),
+            whole([4], 0),
+            whole([5, 6], 0),
+            whole([7], 0),
+            pair(0, 1, 0) + pair(2, 1, 0),
+            pair(0, 1, 1) + pair(2, 1, 1) + whole([4], 1),
+            whole([5, 6, 7], 1),
+            pair(0, 2, 0) + pair(2, 2, 0) + pair(4, 2, 0),
+            pair(0, 2, 1) + pair(2, 2, 1) + pair(4, 2, 1),
+            whole([6, 7], 2),
+            whole(range(0, 7), 3) + [[(7, 3, 0, HALF)], [(7, 3, HALF, P)], [(7, 3, HALF + P, P)]],
         ]
 
         warm(WARM_START)
         waiting = None
         pending = []
-        held = {}
-        for n, (run, plain, block) in enumerate(cycles):
-            ahead = rows_of(cycles[n + 1][0]) if 3 <= n + 1 < len(cycles) else []
-            banks = [transposes(unit) for unit in run]
+        read = []
+        fresh = []
+        for run in runs:
+            fresh.append(sorted({(kind, row) for unit in run for kind, row, g in unit[0]} - set(read)))
+            read += fresh[-1]
+        for n, block in enumerate(blocks):
+            run = runs[n] if n < len(runs) else []
+            ahead = [key for r in range(4, len(runs)) if n == r - (1 if r < 5 else 2) for key in fresh[r]]
+            mine = [key for key in ahead if key[1] % 2 == 0]
+            mine_all = list(mine)
+            banks = []
             baccs = []
-            for c in plain:
-                baccs.append((c, bias_matmul(c)))
+            for i, unit in enumerate(run):
+                if n == 2 and i == 2:
+                    warm(1)
+                banks.append(transposes(unit))
+                if n < 2 and i % 2 == 1:
+                    c = 2 * n + i // 2
+                    baccs.append((c, bias_matmul(c)))
             if waiting is not None:
                 pending.append(add_bias(waiting))
                 waiting = None
-            for key in ahead[0:1]:
-                regroup(nc.vector.tensor_copy, key)
-            tiles = [leave(nc.scalar.copy, bank) for bank in banks[0:3]]
-            for key in ahead[1:2]:
-                regroup(nc.scalar.copy, key)
+            on_vector = [i for i, unit in enumerate(run) if order.index(unit) % 4 == 3]
+            on_scalar = [i for i in range(len(run)) if i not in on_vector]
+            tiles = {}
+            for i in on_scalar:
+                tiles[i] = leave(nc.scalar.copy, banks[i])
+            for key in ahead:
+                if key not in mine_all:
+                    regroup(nc.scalar.copy, key)
             for summed in pending:
                 relu_store(summed)
             pending = []
-            if run:
-                quantise(run[0], tiles[0])
-                tiles.append(leave(nc.vector.tensor_copy, banks[3]))
-                quantise(run[1], tiles[1])
-                quantise(run[2], tiles[2])
-                quantise(run[3], tiles[3])
+            first = 0 if 0 in on_vector else 1
+            for i in on_scalar[0:first]:
+                quantise(run[i], tiles[i])
+            for i in on_vector:
+                tiles[i] = leave(nc.vector.tensor_copy, banks[i])
+            for i in on_scalar[first:] + on_vector:
+                quantise(run[i], tiles[i])
             for c, bacc in baccs:
                 copy = nc.scalar.copy if c % 2 == 0 else nc.vector.tensor_copy
                 copy(out=bias_bc[:, c * CHUNK:(c + 1) * CHUNK], in_=bacc[:])
-            for m, c, lo, width, kind in block:
+            for group in block:
                 if waiting is not None:
                     pending.append(add_bias(waiting))
                     waiting = None
+                    for key in mine[0:1]:
+                        regroup(nc.vector.tensor_copy, key)
+                    mine = mine[1:]
                 if not run:
                     for summed in pending:
                         relu_store(summed)
                     pending = []
-                if kind == "second":
-                    acc = held[(m, c)]
-                else:
-                    acc = acc_pool.tile([P, CHUNK], F32, name="acc")
-                passes(acc, m, c, lo, width)
-                if kind == "first":
-                    held[(m, c)] = acc
-                elif kind == "second":
-                    waiting = (acc, m, c, 0, CHUNK)
-                else:
-                    waiting = (acc, m, c, lo, width)
+                waiting = multiply(group)
+            for key in mine:
+                regroup(nc.vector.tensor_copy, key)
         relu_store(add_bias(waiting))

@@ -191,23 +191,20 @@ def tile_sparselinearrelu_kernel(tc, x, weight, bias, out):
         for c in range(1, N_CHUNKS):
             order += w_half(c, 0) + w_half(c, 1)
 
-        runs = [order[i:i + 4] for i in range(0, 12, 4)] + [order[i:i + 3] for i in range(12, len(order), 3)]
+        runs = [order[i:i + 4] for i in range(0, len(order), 4)]
         blocks = [
             [],
             [],
             pair(0, 0, 0),
             pair(0, 0, 1),
-            whole([2], 0),
-            whole([3], 0),
-            whole([4], 0),
-            whole([5, 6], 0),
-            whole([7], 0),
+            whole([2, 3], 0),
+            whole([4, 5], 0),
+            whole([6, 7], 0),
             pair(0, 1, 0) + pair(2, 1, 0),
             pair(0, 1, 1) + pair(2, 1, 1) + whole([4], 1),
             whole([5, 6, 7], 1),
-            pair(0, 2, 0) + pair(2, 2, 0) + pair(4, 2, 0),
-            pair(0, 2, 1) + pair(2, 2, 1) + pair(4, 2, 1),
-            whole([6, 7], 2),
+            whole(range(0, 4), 2),
+            whole(range(4, 8), 2),
             whole(range(0, 7), 3) + [[(7, 3, 0, HALF)], [(7, 3, HALF, P)], [(7, 3, HALF + P, P)]],
         ]
 
@@ -223,7 +220,6 @@ def tile_sparselinearrelu_kernel(tc, x, weight, bias, out):
             run = runs[n] if n < len(runs) else []
             ahead = [key for r in range(4, len(runs)) if n == r - (1 if r < 5 else 2) for key in fresh[r]]
             mine = [key for key in ahead if key[1] % 2 == 0]
-            mine_all = list(mine)
             banks = []
             baccs = []
             for i, unit in enumerate(run):
@@ -236,13 +232,16 @@ def tile_sparselinearrelu_kernel(tc, x, weight, bias, out):
             if waiting is not None:
                 pending.append(add_bias(waiting))
                 waiting = None
+            for key in mine[0:1]:
+                regroup(nc.vector.tensor_copy, key)
+            mine = mine[1:]
             on_vector = [i for i, unit in enumerate(run) if order.index(unit) % 4 == 3]
             on_scalar = [i for i in range(len(run)) if i not in on_vector]
             tiles = {}
             for i in on_scalar:
                 tiles[i] = leave(nc.scalar.copy, banks[i])
             for key in ahead:
-                if key not in mine_all:
+                if key[1] % 2 == 1:
                     regroup(nc.scalar.copy, key)
             for summed in pending:
                 relu_store(summed)

@@ -61,9 +61,12 @@ def tile_sparselinearrelu_kernel(tc, x, weight, bias, out):
 
         load("w", 0, 2, 2)
         nc.sync.dma_start(out=brow[0:N_CHUNKS, :], in_=bias.rearrange("(o n) -> o n", o=N_CHUNKS))
-        load("x", 0, 2, 2)
-        load("w", 2, 2)
-        for i in range(1, 4):
+        for m in range(2):
+            load("x", m, 1)
+        load("w", 2, 2, 2)
+        for m in range(2, 4):
+            load("x", m, 1)
+        for i in range(2, 4):
             load("x", 2 * i, 2)
         for j in range(4, 16, 2):
             load("w", j, 2)
@@ -235,7 +238,7 @@ def tile_sparselinearrelu_kernel(tc, x, weight, bias, out):
             for key in mine[0:1]:
                 regroup(nc.vector.tensor_copy, key)
             mine = mine[1:]
-            on_vector = [i for i, unit in enumerate(run) if order.index(unit) % 4 == 3]
+            on_vector = [i for i, unit in enumerate(run) if order.index(unit) % 4 == 3 and (n < 3 or n > 7)]
             on_scalar = [i for i in range(len(run)) if i not in on_vector]
             tiles = {}
             for i in on_scalar:
@@ -243,9 +246,10 @@ def tile_sparselinearrelu_kernel(tc, x, weight, bias, out):
             for key in ahead:
                 if key[1] % 2 == 1:
                     regroup(nc.scalar.copy, key)
-            for summed in pending:
+            count = 5 if n >= 8 else 0
+            for summed in pending[0:count]:
                 relu_store(summed)
-            pending = []
+            pending = pending[count:]
             first = 0 if 0 in on_vector else 1
             for i in on_scalar[0:first]:
                 quantise(run[i], tiles[i])

@@ -30,8 +30,8 @@ def tile_sparselinearrelu_kernel(tc, x, weight, bias, out):
         ctx.enter_context(tc.manual_schedule())
         keep = ctx.enter_context(tc.tile_pool(name="keep", bufs=1))
         grp_pool = ctx.enter_context(tc.tile_pool(name="grp", bufs=8))
-        perm_pool = ctx.enter_context(tc.tile_pool(name="permp", bufs=6))
-        st_pool = ctx.enter_context(tc.tile_pool(name="st", bufs=14))
+        perm_pool = ctx.enter_context(tc.tile_pool(name="permp", bufs=5))
+        st_pool = ctx.enter_context(tc.tile_pool(name="st", bufs=16))
         tp_pool = ctx.enter_context(tc.psum_pool(name="tp", bufs=4))
         acc_pool = ctx.enter_context(tc.psum_pool(name="acc", bufs=4))
 
@@ -68,8 +68,16 @@ def tile_sparselinearrelu_kernel(tc, x, weight, bias, out):
             load("x", m, 1)
         for i in range(2, 4):
             load("x", 2 * i, 2)
-        for j in range(4, 16, 2):
+        for j in range(4, 12, 2):
             load("w", j, 2)
+
+        w_quad = weight.rearrange("(j i r) (g q) -> j i (r g) q", j=K // P, r=4, g=PASSES)
+        quad = {}
+        for j in range(12, 16):
+            t = keep.tile([P, 4 * PASSES, P], BF16, name="w_quad_%d" % j)
+            for a in (0, 2, 1, 3):
+                nc.sync.dma_start(out=t[32 * a:32 * a + 32, :, :], in_=w_quad[j, :, :, P * a:P * a + P])
+            quad[j] = t
 
         xq = [keep.tile([P, PASSES * P], U32, name="xq_%d" % m, align_bytes=64) for m in range(M_TILES)]
         xs = [keep.tile([P, PASSES * P], U8, name="xs_%d" % m, align_bytes=64) for m in range(M_TILES)]
@@ -160,11 +168,21 @@ def tile_sparselinearrelu_kernel(tc, x, weight, bias, out):
             m, c, lo, width = group[0]
             n = len(group)
             st = st_pool.tile([P, CHUNK], F32, name="st")
-            nc.vector.tensor_tensor(
-                out=st[:, 0:n * width].rearrange("p (n w) -> p n w", n=n),
-                in0=acc[:, 0:n * width].rearrange("p (n w) -> p n w", n=n),
-                in1=bias_bc[:, c * CHUNK + lo:c * CHUNK + lo + width].unsqueeze(1).to_broadcast([P, n, width]),
-                op=ADD)
+            values = bias_bc[:, c * CHUNK + lo:c * CHUNK + lo + width]
+            if c == N_CHUNKS - 1:
+                for part in range(n):
+                    cols = slice(width * part, width * part + width)
+                    nc.vector.tensor_tensor(
+                        out=st[:, cols].rearrange("p (j i r) -> p j i r", i=32, r=4),
+                        in0=acc[:, cols].rearrange("p (j r i) -> p j i r", i=32, r=4),
+                        in1=values.rearrange("p (j i r) -> p j i r", i=32, r=4),
+                        op=ADD)
+            else:
+                nc.vector.tensor_tensor(
+                    out=st[:, 0:n * width].rearrange("p (n w) -> p n w", n=n),
+                    in0=acc[:, 0:n * width].rearrange("p (n w) -> p n w", n=n),
+                    in1=values.unsqueeze(1).to_broadcast([P, n, width]),
+                    op=ADD)
             return st, group
 
         def relu_store(summed):
@@ -175,6 +193,39 @@ def tile_sparselinearrelu_kernel(tc, x, weight, bias, out):
             for m, c, lo, width in group:
                 nc.sync.dma_start(out=out_view[m][:, c * CHUNK + lo:c * CHUNK + lo + width], in_=st[:, at:at + width])
                 at += width
+
+        halfway = {}
+        joined = {}
+
+        def split(j, engine_copy):
+            t = perm_pool.tile([P, C], BF16, name="perm", align_bytes=64)
+            engine_copy(
+                out=t[:].bitcast(F32).rearrange("p (b u l) -> p b u l", u=2, l=32),
+                in_=quad[j][:].rearrange("p b q -> p (b q)").bitcast(F32).rearrange("p (b l u) -> p b u l", l=32, u=2),
+            )
+            halfway[j] = t
+
+        def turn(j):
+            t = perm_pool.tile([P, C], BF16, name="perm", align_bytes=64)
+            nc.vector.transpose(t[:].bitcast(F32), halfway[j][:].bitcast(F32))
+            halfway[j] = t
+
+        def join(j, engine_copy):
+            joined[j] = []
+            for g in range(PASSES):
+                if g % 2 == 0:
+                    pair_of_passes = grp_pool.tile([P, 1024], BF16, name="grouped", align_bytes=64)
+                part = pair_of_passes[:, 512 * (g % 2):512 * (g % 2) + 512]
+                engine_copy(
+                    out=part.bitcast(F32).rearrange("p (r i u) -> p r i u", r=4, u=2),
+                    in_=halfway[j][:].bitcast(F32).rearrange("p (r g u i) -> p g r i u", r=4, g=PASSES, u=2)[:, g],
+                )
+                joined[j].append(part)
+
+        def quantise_tile(j):
+            cols = slice(P * (j - 12), P * (j - 12) + P)
+            for g in range(PASSES):
+                nc.vector.quantize_mx(out=wq[3][g][:, cols].bitcast(FP8X4), scales=ws[3][g][:, cols], in_=joined[j][g])
 
         def w_half(c, h):
             return [w_unit(c, h, g) for g in range(PASSES)]
@@ -191,7 +242,7 @@ def tile_sparselinearrelu_kernel(tc, x, weight, bias, out):
         order = w_half(0, 0) + x_tile(0) + x_tile(1) + w_half(0, 1)
         for m in range(2, M_TILES):
             order += x_tile(m)
-        for c in range(1, N_CHUNKS):
+        for c in range(1, N_CHUNKS - 1):
             order += w_half(c, 0) + w_half(c, 1)
 
         runs = [order[i:i + 4] for i in range(0, len(order), 4)]
@@ -206,10 +257,37 @@ def tile_sparselinearrelu_kernel(tc, x, weight, bias, out):
             pair(0, 1, 0) + pair(2, 1, 0),
             pair(0, 1, 1) + pair(2, 1, 1) + whole([4], 1),
             whole([5, 6, 7], 1),
-            whole(range(0, 4), 2),
-            whole(range(4, 8), 2),
-            whole(range(0, 7), 3) + [[(7, 3, 0, HALF)], [(7, 3, HALF, P)], [(7, 3, HALF + P, P)]],
+            whole(range(0, 8), 2)
+            + pair(0, 3, 0) + pair(2, 3, 0) + pair(4, 3, 0) + pair(6, 3, 0)
+            + pair(0, 3, 1) + pair(2, 3, 1) + pair(4, 3, 1)
+            + [[(6, 3, HALF, HALF)], [(7, 3, HALF, P)], [(7, 3, HALF + P, P)]],
         ]
+
+        side = {
+            ("run", 8): [("split", 12, "scalar"), ("split", 13, "scalar")],
+            ("end", 8): [("turn", 12, "vector")],
+            ("run", 9): [("join", 12, "scalar"), ("turn", 13, "vector")],
+            ("bank", 0): [("quantise", 12, "vector"), ("join", 13, "scalar")],
+            ("bank", 1): [("split", 14, "scalar")],
+            ("bank", 2): [("quantise", 13, "vector"), ("split", 15, "scalar")],
+            ("bank", 3): [("turn", 14, "vector")],
+            ("bank", 5): [("turn", 15, "vector"), ("join", 14, "scalar")],
+            ("bank", 7): [("quantise", 14, "vector")],
+            ("bank", 8): [("join", 15, "vector")],
+            ("bank", 10): [("quantise", 15, "vector")],
+        }
+
+        def do_side(at):
+            for step, j, engine in side.get(at, []):
+                copy = nc.scalar.copy if engine == "scalar" else nc.vector.tensor_copy
+                if step == "split":
+                    split(j, copy)
+                if step == "turn":
+                    turn(j)
+                if step == "join":
+                    join(j, copy)
+                if step == "quantise":
+                    quantise_tile(j)
 
         warm(WARM_START)
         waiting = None
@@ -226,8 +304,6 @@ def tile_sparselinearrelu_kernel(tc, x, weight, bias, out):
             banks = []
             baccs = []
             for i, unit in enumerate(run):
-                if n == 2 and i == 2:
-                    warm(1)
                 banks.append(transposes(unit))
                 if n < 2 and i % 2 == 1:
                     c = 2 * n + i // 2
@@ -238,7 +314,7 @@ def tile_sparselinearrelu_kernel(tc, x, weight, bias, out):
             for key in mine[0:1]:
                 regroup(nc.vector.tensor_copy, key)
             mine = mine[1:]
-            on_vector = [i for i, unit in enumerate(run) if order.index(unit) % 4 == 3 and (n < 3 or n > 7)]
+            on_vector = [i for i, unit in enumerate(run) if order.index(unit) % 4 == 3]
             on_scalar = [i for i in range(len(run)) if i not in on_vector]
             tiles = {}
             for i in on_scalar:
@@ -246,7 +322,7 @@ def tile_sparselinearrelu_kernel(tc, x, weight, bias, out):
             for key in ahead:
                 if key[1] % 2 == 1:
                     regroup(nc.scalar.copy, key)
-            count = 5 if n >= 8 else 0
+            count = len(pending) if run else 0
             for summed in pending[0:count]:
                 relu_store(summed)
             pending = pending[count:]
@@ -260,18 +336,23 @@ def tile_sparselinearrelu_kernel(tc, x, weight, bias, out):
             for c, bacc in baccs:
                 copy = nc.scalar.copy if c % 2 == 0 else nc.vector.tensor_copy
                 copy(out=bias_bc[:, c * CHUNK:(c + 1) * CHUNK], in_=bacc[:])
-            for group in block:
+            do_side(("run", n))
+            for k, group in enumerate(block):
                 if waiting is not None:
                     pending.append(add_bias(waiting))
                     waiting = None
                     for key in mine[0:1]:
                         regroup(nc.vector.tensor_copy, key)
                     mine = mine[1:]
-                if not run:
-                    for summed in pending:
+                if not run and k >= 3:
+                    for summed in pending[0:2]:
                         relu_store(summed)
-                    pending = []
+                    pending = pending[2:]
+                if not run:
+                    do_side(("bank", k))
                 waiting = multiply(group)
             for key in mine:
                 regroup(nc.vector.tensor_copy, key)
-        relu_store(add_bias(waiting))
+            do_side(("end", n))
+        for summed in pending + [add_bias(waiting)]:
+            relu_store(summed)

from contextlib import ExitStack

import concourse.mybir as mybir
from concourse.masks import make_identity

F32 = mybir.dt.float32
BF16 = mybir.dt.bfloat16
I32 = mybir.dt.int32
U32 = mybir.dt.uint32
U8 = mybir.dt.uint8
FP8X4 = mybir.dt.float8_e4m3fn_x4
ADD = mybir.AluOpType.add
RELU = mybir.ActivationFunctionType.Relu

P = 128
B, C, K = 1024, 2048, 2048
FLOPS = 2 * B * C * K

M_TILES = B // P
CHUNK = 512
HALF = CHUNK // 2
N_CHUNKS = K // CHUNK
PASSES = C // 512
WARM_START = 5


def tile_sparselinearrelu_kernel(tc, x, weight, bias, out):
    nc = tc.nc
    with ExitStack() as ctx:
        ctx.enter_context(tc.manual_schedule())
        keep = ctx.enter_context(tc.tile_pool(name="keep", bufs=1))
        grp_pool = ctx.enter_context(tc.tile_pool(name="grp", bufs=8))
        perm_pool = ctx.enter_context(tc.tile_pool(name="permp", bufs=5))
        st_pool = ctx.enter_context(tc.tile_pool(name="st", bufs=16))
        tp_pool = ctx.enter_context(tc.psum_pool(name="tp", bufs=4))
        acc_pool = ctx.enter_context(tc.psum_pool(name="acc", bufs=4))

        x_view = x.rearrange("(p t) k -> p t k", t=M_TILES)
        out_view = out.rearrange("(p t) n -> t p n", t=M_TILES)
        w_view = weight.rearrange("(j p) k -> p j k", p=P)

        brow = keep.tile([P, CHUNK], BF16, name="brow")
        nc.vector.memset(brow[:].bitcast(I32), 0)
        ones = keep.tile([P, CHUNK], BF16, name="ones")
        nc.vector.memset(ones[:], 1.0)
        ident = keep.tile([P, P], F32, name="ident")
        make_identity(nc, ident[:])
        pick = keep.tile([P, N_CHUNKS], BF16, name="pick")
        nc.vector.tensor_copy(out=pick[:], in_=ident[:, 0:N_CHUNKS])

        raw = {}

        def load(kind, first, count, parts=1):
            view = x_view if kind == "x" else w_view
            width = C // parts
            for i in range(parts):
                t = keep.tile([P, count, width], BF16, name="%s_sb_%d_%d" % (kind, first, i))
                nc.sync.dma_start(out=t[:], in_=view[:, first:first + count, width * i:width * i + width])
                for j in range(count):
                    raw.setdefault((kind, first + j), []).append(t[:, j, :])

        load("w", 0, 2, 2)
        nc.sync.dma_start(out=brow[0:N_CHUNKS, :], in_=bias.rearrange("(o n) -> o n", o=N_CHUNKS))
        for m in range(2):
            load("x", m, 1)
        load("w", 2, 2, 2)
        for m in range(2, 4):
            load("x", m, 1)
        for i in range(2, 4):
            load("x", 2 * i, 2)
        for j in range(4, 12, 2):
            load("w", j, 2)

        w_quad = weight.rearrange("(j i r) (g q) -> j i (r g) q", j=K // P, r=4, g=PASSES)
        quad = {}
        for j in range(12, 16):
            t = keep.tile([P, 4 * PASSES, P], BF16, name="w_quad_%d" % j)
            for a in (0, 2, 1, 3):
                nc.sync.dma_start(out=t[32 * a:32 * a + 32, :, :], in_=w_quad[j, :, :, P * a:P * a + P])
            quad[j] = t

        xq = [keep.tile([P, PASSES * P], U32, name="xq_%d" % m, align_bytes=64) for m in range(M_TILES)]
        xs = [keep.tile([P, PASSES * P], U8, name="xs_%d" % m, align_bytes=64) for m in range(M_TILES)]
        wq = [[keep.tile([P, CHUNK], U32, name="wq_%d_%d" % (c, g), align_bytes=64) for g in range(PASSES)]
              for c in range(N_CHUNKS)]
        ws = [[keep.tile([P, CHUNK], U8, name="ws_%d_%d" % (c, g), align_bytes=64) for g in range(PASSES)]
              for c in range(N_CHUNKS)]
        bias_bc = keep.tile([P, K], F32, name="bias_bc")

        def warm(n):
            for i in range(n):
                wacc = acc_pool.tile([P, CHUNK], F32, name="acc")
                nc.tensor.matmul(out=wacc[:], lhsT=ones[:, 0:P], rhs=ones[:], start=True, stop=True)

        def bias_matmul(c):
            bacc = acc_pool.tile([P, CHUNK], F32, name="acc")
            nc.tensor.matmul(out=bacc[:], lhsT=pick[:, c:c + 1].to_broadcast([P, P]), rhs=brow[:],
                             start=True, stop=True)
            return bacc

        perm = {}

        def regroup(engine_copy, key):
            t = perm_pool.tile([P, C], BF16, name="perm", align_bytes=64)
            engine_copy(
                out=t[:].bitcast(F32).rearrange("p (g u c) -> p g u c", g=PASSES, u=2),
                in_=raw[key][0].bitcast(F32).rearrange("p (g c u) -> p g u c", g=PASSES, u=2),
            )
            perm[key] = t

        def words(key, g, u):
            if key in perm:
                return perm[key][:].bitcast(F32)[:, 256 * g + P * u:256 * g + P * u + P]
            parts = raw[key]
            per_part = PASSES // len(parts)
            lo = 256 * (g % per_part)
            return parts[g // per_part].bitcast(F32)[:, lo + u:lo + 256:2]

        def w_unit(c, h, g):
            srcs = [("w", 4 * c + 2 * h + j, g) for j in range(2)]
            cols = slice(HALF * h, HALF * h + HALF)
            return srcs, wq[c][g][:, cols], ws[c][g][:, cols]

        def x_unit(m, gp):
            srcs = [("x", m, 2 * gp + a) for a in range(2)]
            cols = slice(256 * gp, 256 * gp + 256)
            return srcs, xq[m][:, cols], xs[m][:, cols]

        def transposes(unit):
            bank = tp_pool.tile([P, 2, 2, P], F32, name="bank")
            for a in range(2):
                kind, row, g = unit[0][a]
                for u in range(2):
                    nc.tensor.transpose(bank[:, a, u, :], words((kind, row), g, u), ident[:])
            return bank

        def leave(engine_copy, bank):
            grouped = grp_pool.tile([P, 1024], BF16, name="grouped", align_bytes=64)
            engine_copy(
                out=grouped[:].bitcast(F32).rearrange("p (a c u) -> p a c u", a=2, u=2),
                in_=bank[:].rearrange("p a u c -> p a c u"),
            )
            return grouped

        def quantise(unit, grouped):
            nc.vector.quantize_mx(out=unit[1].bitcast(FP8X4), scales=unit[2], in_=grouped[:])

        def multiply(group):
            acc = acc_pool.tile([P, CHUNK], F32, name="acc")
            at = 0
            for m, c, lo, width in group:
                for g in range(PASSES):
                    cols = slice(P * g, P * g + P)
                    nc.tensor.matmul_mx(
                        out=acc[:, at:at + width],
                        lhsT=xq[m][:, cols].bitcast(FP8X4),
                        lhsT_scale=xs[m][:, cols],
                        rhs=wq[c][g][:, lo:lo + width].bitcast(FP8X4),
                        rhs_scale=ws[c][g][:, lo:lo + width],
                        start=(g == 0),
                        stop=(g == PASSES - 1),
                    )
                at += width
            return acc, group

        def add_bias(done):
            acc, group = done
            m, c, lo, width = group[0]
            n = len(group)
            st = st_pool.tile([P, CHUNK], F32, name="st")
            values = bias_bc[:, c * CHUNK + lo:c * CHUNK + lo + width]
            if c == N_CHUNKS - 1:
                for part in range(n):
                    cols = slice(width * part, width * part + width)
                    nc.vector.tensor_tensor(
                        out=st[:, cols].rearrange("p (j i r) -> p j i r", i=32, r=4),
                        in0=acc[:, cols].rearrange("p (j r i) -> p j i r", i=32, r=4),
                        in1=values.rearrange("p (j i r) -> p j i r", i=32, r=4),
                        op=ADD)
            else:
                nc.vector.tensor_tensor(
                    out=st[:, 0:n * width].rearrange("p (n w) -> p n w", n=n),
                    in0=acc[:, 0:n * width].rearrange("p (n w) -> p n w", n=n),
                    in1=values.unsqueeze(1).to_broadcast([P, n, width]),
                    op=ADD)
            return st, group

        def relu_store(summed):
            st, group = summed
            total = sum(width for m, c, lo, width in group)
            nc.scalar.activation(out=st[:, 0:total], in_=st[:, 0:total], func=RELU)
            at = 0
            for m, c, lo, width in group:
                nc.sync.dma_start(out=out_view[m][:, c * CHUNK + lo:c * CHUNK + lo + width], in_=st[:, at:at + width])
                at += width

        halfway = {}
        joined = {}

        def split(j, engine_copy):
            t = perm_pool.tile([P, C], BF16, name="perm", align_bytes=64)
            engine_copy(
                out=t[:].bitcast(F32).rearrange("p (b u l) -> p b u l", u=2, l=32),
                in_=quad[j][:].rearrange("p b q -> p (b q)").bitcast(F32).rearrange("p (b l u) -> p b u l", l=32, u=2),
            )
            halfway[j] = t

        def turn(j):
            t = perm_pool.tile([P, C], BF16, name="perm", align_bytes=64)
            nc.vector.transpose(t[:].bitcast(F32), halfway[j][:].bitcast(F32))
            halfway[j] = t

        def join(j, engine_copy):
            joined[j] = []
            for g in range(PASSES):
                if g % 2 == 0:
                    pair_of_passes = grp_pool.tile([P, 1024], BF16, name="grouped", align_bytes=64)
                part = pair_of_passes[:, 512 * (g % 2):512 * (g % 2) + 512]
                engine_copy(
                    out=part.bitcast(F32).rearrange("p (r i u) -> p r i u", r=4, u=2),
                    in_=halfway[j][:].bitcast(F32).rearrange("p (r g u i) -> p g r i u", r=4, g=PASSES, u=2)[:, g],
                )
                joined[j].append(part)

        def quantise_tile(j):
            cols = slice(P * (j - 12), P * (j - 12) + P)
            for g in range(PASSES):
                nc.vector.quantize_mx(out=wq[3][g][:, cols].bitcast(FP8X4), scales=ws[3][g][:, cols], in_=joined[j][g])

        def w_half(c, h):
            return [w_unit(c, h, g) for g in range(PASSES)]

        def x_tile(m):
            return [x_unit(m, gp) for gp in range(2)]

        def whole(ms, c):
            return [[(m, c, 0, CHUNK)] for m in ms]

        def pair(m, c, h):
            return [[(m, c, HALF * h, HALF), (m + 1, c, HALF * h, HALF)]]

        order = w_half(0, 0) + x_tile(0) + x_tile(1) + w_half(0, 1)
        for m in range(2, M_TILES):
            order += x_tile(m)
        for c in range(1, N_CHUNKS - 1):
            order += w_half(c, 0) + w_half(c, 1)

        runs = [order[i:i + 4] for i in range(0, len(order), 4)]
        blocks = [
            [],
            [],
            pair(0, 0, 0),
            pair(0, 0, 1),
            whole([2, 3], 0),
            whole([4, 5], 0),
            whole([6, 7], 0),
            pair(0, 1, 0) + pair(2, 1, 0),
            pair(0, 1, 1) + pair(2, 1, 1) + whole([4], 1),
            whole([5, 6, 7], 1),
            whole(range(0, 8), 2)
            + pair(0, 3, 0) + pair(2, 3, 0) + pair(4, 3, 0) + pair(6, 3, 0)
            + pair(0, 3, 1) + pair(2, 3, 1) + pair(4, 3, 1)
            + [[(6, 3, HALF, HALF)], [(7, 3, HALF, P)], [(7, 3, HALF + P, P)]],
        ]

        side = {
            ("run", 8): [("split", 12, "scalar"), ("split", 13, "scalar")],
            ("end", 8): [("turn", 12, "vector")],
            ("run", 9): [("join", 12, "scalar"), ("turn", 13, "vector")],
            ("bank", 0): [("quantise", 12, "vector"), ("join", 13, "scalar")],
            ("bank", 1): [("split", 14, "scalar")],
            ("bank", 2): [("quantise", 13, "vector"), ("split", 15, "scalar")],
            ("bank", 3): [("turn", 14, "vector")],
            ("bank", 5): [("turn", 15, "vector"), ("join", 14, "scalar")],
            ("bank", 7): [("quantise", 14, "vector")],
            ("bank", 8): [("join", 15, "vector")],
            ("bank", 10): [("quantise", 15, "vector")],
        }

        def do_side(at):
            for step, j, engine in side.get(at, []):
                copy = nc.scalar.copy if engine == "scalar" else nc.vector.tensor_copy
                if step == "split":
                    split(j, copy)
                if step == "turn":
                    turn(j)
                if step == "join":
                    join(j, copy)
                if step == "quantise":
                    quantise_tile(j)

        warm(WARM_START)
        waiting = None
        pending = []
        read = []
        fresh = []
        for run in runs:
            fresh.append(sorted({(kind, row) for unit in run for kind, row, g in unit[0]} - set(read)))
            read += fresh[-1]
        for n, block in enumerate(blocks):
            run = runs[n] if n < len(runs) else []
            ahead = [key for r in range(4, len(runs)) if n == r - (1 if r < 5 else 2) for key in fresh[r]]
            mine = [key for key in ahead if key[1] % 2 == 0]
            banks = []
            baccs = []
            for i, unit in enumerate(run):
                banks.append(transposes(unit))
                if n < 2 and i % 2 == 1:
                    c = 2 * n + i // 2
                    baccs.append((c, bias_matmul(c)))
            if waiting is not None:
                pending.append(add_bias(waiting))
                waiting = None
            for key in mine[0:1]:
                regroup(nc.vector.tensor_copy, key)
            mine = mine[1:]
            on_vector = [i for i, unit in enumerate(run) if order.index(unit) % 4 == 3]
            on_scalar = [i for i in range(len(run)) if i not in on_vector]
            tiles = {}
            for i in on_scalar:
                tiles[i] = leave(nc.scalar.copy, banks[i])
            for key in ahead:
                if key[1] % 2 == 1:
                    regroup(nc.scalar.copy, key)
            count = len(pending) if run else 0
            for summed in pending[0:count]:
                relu_store(summed)
            pending = pending[count:]
            first = 0 if 0 in on_vector else 1
            for i in on_scalar[0:first]:
                quantise(run[i], tiles[i])
            for i in on_vector:
                tiles[i] = leave(nc.vector.tensor_copy, banks[i])
            for i in on_scalar[first:] + on_vector:
                quantise(run[i], tiles[i])
            for c, bacc in baccs:
                copy = nc.scalar.copy if c % 2 == 0 else nc.vector.tensor_copy
                copy(out=bias_bc[:, c * CHUNK:(c + 1) * CHUNK], in_=bacc[:])
            do_side(("run", n))
            for k, group in enumerate(block):
                if waiting is not None:
                    pending.append(add_bias(waiting))
                    waiting = None
                    for key in mine[0:1]:
                        regroup(nc.vector.tensor_copy, key)
                    mine = mine[1:]
                if not run and k >= 3:
                    for summed in pending[0:2]:
                        relu_store(summed)
                    pending = pending[2:]
                if not run:
                    do_side(("bank", k))
                waiting = multiply(group)
            for key in mine:
                regroup(nc.vector.tensor_copy, key)
            do_side(("end", n))
        for summed in pending + [add_bias(waiting)]:
            relu_store(summed)
